import numpy as np
import ml_dtypes


def mxq(x, axis, fmt="e4m3"):
    dtype, down = {"e4m3": (ml_dtypes.float8_e4m3fn, 7), "e5m2": (ml_dtypes.float8_e5m2, 14)}[fmt]
    v = np.moveaxis(np.asarray(x, np.float32).astype(ml_dtypes.bfloat16).astype(np.float64), axis, -1)
    blocks = v.reshape(v.shape[:-1] + (-1, 32))
    amax = np.abs(blocks).max(-1, keepdims=True)
    byte = np.maximum(np.where(amax > 0, np.frexp(amax)[1] - 1 + 127, 0) - down, 1)
    scale = np.exp2(byte - 127.0)
    codes = (blocks / scale).astype(np.float32).astype(dtype).astype(np.float64)
    return np.moveaxis((codes * scale).reshape(v.shape), -1, axis)


WIDE = False


def mx_kscale(k):
    if not WIDE:
        return np.ones(k)
    levels = np.array([10, -10, 5, -5, 0])
    if k % 512:
        return np.exp2(np.random.permutation(np.resize(levels, k // 32))).repeat(32)
    a = np.empty((k // 512, 16))
    for p in range(k // 512):
        a[p, :8] = np.random.permutation(np.resize(levels, 8))
        for g in range(8):
            far = levels[np.abs(levels - a[p, g]) >= 10]
            a[p, g + 8] = far[np.random.randint(len(far))]
    return np.exp2(a.ravel()).repeat(32)


BF16 = ml_dtypes.bfloat16


def bf(x):
    return np.asarray(x, np.float32).astype(BF16)


def f64(x):
    return np.asarray(x).astype(np.float64)


B, H = 4096, 512


def sigmoid(v):
    return 1.0 / (1.0 + np.exp(-v))


def setup_inputs():
    s = mx_kscale(H)
    w = lambda: bf(np.random.standard_normal((H, H)) * 0.7 / np.sqrt(H) / s[None, :])
    b = lambda: bf(np.random.standard_normal(H) * 0.5)
    return {"inputs": bf(np.random.standard_normal((B, H)) * s),
            "short_term_memory": bf(np.random.standard_normal((B, H)) * s),
            "Wf": w(), "b_f": b(), "Wi": w(), "b_i": b(), "Wg": w(), "b_g": b(), "Wo": w(), "b_o": b()}


def reference(inputs, short_term_memory, Wf, b_f, Wi, b_i, Wg, b_g, Wo, b_o):
    z = f64(inputs) + f64(short_term_memory)
    zq = mxq(z, 1, "e4m3")
    c = sigmoid((zq @ mxq(f64(Wf), 1, "e4m3").T) + f64(b_f))
    c = c + sigmoid((zq @ mxq(f64(Wi), 1, "e4m3").T) + f64(b_i)) * np.tanh((zq @ mxq(f64(Wg), 1, "e4m3").T) + f64(b_g))
    h = np.tanh(c) * sigmoid((zq @ mxq(f64(Wo), 1, "e4m3").T) + f64(b_o))
    return np.stack((c, h))

@@ -1,0 +1,308 @@
+from contextlib import ExitStack
+
+import concourse.mybir as mybir
+from concourse.masks import make_identity
+
+F32 = mybir.dt.float32
+BF16 = mybir.dt.bfloat16
+U32 = mybir.dt.uint32
+U8 = mybir.dt.uint8
+FP8X4 = mybir.dt.float8_e4m3fn_x4
+ACT = mybir.ActivationFunctionType
+ALU = mybir.AluOpType
+
+B = 4096
+H = 512
+P = 128
+GATES = 4
+I_GATE = 0
+G_GATE = 1
+F_GATE = 2
+O_GATE = 3
+ROUND = 512
+CHUNKS = H // P
+BLOCKS = ROUND // P
+STEPS = (B // ROUND) * CHUNKS
+PARITIES = 2
+UNIT = 2
+UNIT_COLS = UNIT * P
+PAIRS = BLOCKS // UNIT
+GATE_UNITS = GATES // UNIT
+Z_UNITS = B // (UNIT * P)
+FIRST_UNITS = PAIRS
+FIRST_CHUNKS = 2
+LEAD = 6
+LOADS_AHEAD = 4
+LAST_LAG = 4
+
+FLOPS = 2 * B * H * GATES * H
+
+
+def tile_lstmcell_pa_t_kernel(
+    tc, inputs, short_term_memory, Wf, b_f, Wi, b_i, Wg, b_g, Wo, b_o, out
+):
+    nc = tc.nc
+    weights = [Wi, Wg, Wf, Wo]
+    biases = [b_i, b_g, b_f, b_o]
+    functions = [ACT.Sigmoid, ACT.Tanh, ACT.Sigmoid, ACT.Sigmoid]
+    gate_names = ["sig_i", "tanh_g", "sig_f", "sig_o"]
+    x_view = inputs.rearrange("(r p a t) k -> r a p t k", p=P, a=PAIRS, t=UNIT)
+    h_view = short_term_memory.rearrange("(r p a t) k -> r a p t k", p=P, a=PAIRS, t=UNIT)
+    out_view = out.rearrange("o (r p s) (m f) -> o r m p s f", p=P, s=BLOCKS, f=P)
+
+    with ExitStack() as ctx:
+        keep = ctx.enter_context(tc.tile_pool(name="keep", bufs=1))
+        loads = ctx.enter_context(tc.tile_pool(name="loads", bufs=LOADS_AHEAD))
+        prep = ctx.enter_context(tc.tile_pool(name="prep", bufs=3))
+        w_prep = ctx.enter_context(tc.tile_pool(name="w_prep", bufs=FIRST_CHUNKS * GATE_UNITS))
+        gate_pool = ctx.enter_context(tc.tile_pool(name="gates", bufs=LAST_LAG + 1))
+        cell_pool = ctx.enter_context(tc.tile_pool(name="cells", bufs=3))
+        result_pool = ctx.enter_context(tc.tile_pool(name="results", bufs=4))
+        acc_pool = ctx.enter_context(tc.psum_pool(name="acc", bufs=GATES))
+        cell_bank = ctx.enter_context(tc.psum_pool(name="cell_bank", bufs=1))
+        turn_pool = ctx.enter_context(tc.psum_pool(name="turned", bufs=3))
+
+        ident = keep.tile([P, P], F32, name="ident")
+        make_identity(nc, ident[:])
+
+        ctx.enter_context(tc.manual_schedule())
+
+        w_raw = keep.tile([P, CHUNKS, GATES, H], BF16, name="w_raw")
+        w_codes = keep.tile([P, CHUNKS, GATES, P], U32, name="w_codes", align_bytes=64)
+        w_scales = keep.tile([P, CHUNKS, GATES, P], U8, name="w_scales", align_bytes=64)
+        bias_rows = keep.tile([P, P], BF16, name="bias_rows")
+        bias_rows_f32 = keep.tile([P, P], F32, name="bias_rows_f32")
+        bias = keep.tile([P, GATES * CHUNKS], F32, name="bias")
+        zero = keep.tile([P, 1], F32, name="zero")
+        half = keep.tile([P, 1], F32, name="half")
+
+        w_turned = {}
+        w_grouped = {}
+        x_raw = {}
+        h_raw = {}
+        z_sum = {}
+        z_turned = {}
+        z_grouped = {}
+        z_codes = {}
+        z_scales = {}
+        acc = {}
+        gate = {}
+        product = {}
+        cell_t = {}
+        cell_rows = {}
+        sig_o_rows = {}
+        cell = {}
+        tanh_c = {}
+
+
+        def turn(source):
+            turned = turn_pool.tile([P, UNIT, PARITIES, P], F32, name="unit_turned", tag="turned")
+            for t in range(UNIT):
+                words = source[:, t, :].bitcast(F32)
+                for u in range(PARITIES):
+                    nc.tensor.transpose(turned[:, t, u, :], words[:, u :: PARITIES], ident[:])
+            return turned
+
+        def group(turned, pool, copy):
+            grouped = pool.tile([P, UNIT * H], BF16, name="grouped", align_bytes=64)
+            copy(
+                out=grouped[:].bitcast(F32).rearrange("p (t c u) -> p t c u", t=UNIT, u=PARITIES),
+                in_=turned[:].rearrange("p t u c -> p t c u"),
+            )
+            return grouped
+
+        def quantise(grouped, codes, scales):
+            nc.vector.quantize_mx(out=codes.bitcast(FP8X4), scales=scales, in_=grouped[:])
+
+
+        def load_weights(m):
+            for g in range(GATES):
+                nc.sync.dma_start(out=w_raw[:, m, g, :], in_=weights[g][m * P : (m + 1) * P, :])
+
+        def turn_weights(m):
+            w_turned[m] = [
+                turn(w_raw[:, m, v * UNIT : (v + 1) * UNIT, :]) for v in range(GATE_UNITS)
+            ]
+
+        def group_weights(m, copy):
+            w_grouped[m] = [group(turned, w_prep, copy) for turned in w_turned[m]]
+
+        def quantise_weights(m):
+            for v in range(GATE_UNITS):
+                gates_of_unit = slice(v * UNIT, (v + 1) * UNIT)
+                quantise(
+                    w_grouped[m][v],
+                    w_codes[:, m, gates_of_unit, :].rearrange("p g o -> p (g o)"),
+                    w_scales[:, m, gates_of_unit, :].rearrange("p g o -> p (g o)"),
+                )
+
+        def load_biases():
+            nc.vector.memset(bias_rows[:], 0.0)
+            for g in range(GATES):
+                nc.scalar.dma_start(
+                    out=bias_rows[g * CHUNKS : (g + 1) * CHUNKS, :],
+                    in_=biases[g].rearrange("(m c) -> m c", c=P),
+                )
+
+
+        def load_unit(q):
+            r, a = divmod(q, PAIRS)
+            x_raw[q] = loads.tile([P, UNIT, H], BF16, name="x_raw")
+            nc.sync.dma_start(out=x_raw[q][:], in_=x_view[r, a])
+            h_raw[q] = loads.tile([P, UNIT, H], BF16, name="h_raw")
+            nc.sync.dma_start(out=h_raw[q][:], in_=h_view[r, a])
+
+        def add_z(q):
+            z_sum[q] = prep.tile([P, UNIT, H], BF16, name="z_sum")
+            nc.vector.tensor_tensor(out=z_sum[q][:], in0=x_raw[q][:], in1=h_raw[q][:], op=ALU.add)
+            if q + LOADS_AHEAD < Z_UNITS:
+                load_unit(q + LOADS_AHEAD)
+
+        def quantise_z(q):
+            r, a = divmod(q, PAIRS)
+            if a == 0:
+                z_codes[r] = prep.tile([P, ROUND], U32, name="z_codes", align_bytes=64)
+                z_scales[r] = prep.tile([P, ROUND], U8, name="z_scales", align_bytes=64)
+            columns = slice(a * UNIT_COLS, (a + 1) * UNIT_COLS)
+            quantise(z_grouped[q], z_codes[r][:, columns], z_scales[r][:, columns])
+
+
+        def multiply(n):
+            r, m = divmod(n, CHUNKS)
+            for g in range(GATES):
+                acc[n, g] = acc_pool.tile([P, ROUND], F32, name="acc")
+                nc.tensor.matmul_mx(
+                    out=acc[n, g][:],
+                    lhsT=w_codes[:, m, g, :].bitcast(FP8X4),
+                    lhsT_scale=w_scales[:, m, g, :],
+                    rhs=z_codes[r][:].bitcast(FP8X4),
+                    rhs_scale=z_scales[r][:],
+                    start=True,
+                    stop=True,
+                )
+
+        def activate(n, g):
+            gate[n, g] = gate_pool.tile([P, ROUND], F32, name=gate_names[g])
+            column = g * CHUNKS + n % CHUNKS
+            nc.scalar.activation(
+                out=gate[n, g][:],
+                in_=acc[n, g][:],
+                func=functions[g],
+                bias=bias[:, column : column + 1],
+                scale=1.0,
+            )
+
+        def multiply_gates(n):
+            product[n] = cell_pool.tile([P, ROUND], F32, name="product")
+            nc.gpsimd.tensor_tensor(
+                out=product[n][:], in0=gate[n, I_GATE][:], in1=gate[n, G_GATE][:], op=ALU.mult
+            )
+
+        def add_cell(n):
+            cell_t[n] = cell_pool.tile([P, ROUND], F32, name="cell_t")
+            nc.vector.tensor_tensor(
+                out=cell_t[n][:], in0=gate[n, F_GATE][:], in1=product[n][:], op=ALU.add
+            )
+
+        def turn_back(rows, source):
+            for s in range(BLOCKS):
+                nc.tensor.transpose(rows[:, s, :], source[:, s * P : (s + 1) * P], ident[:])
+
+        def turn_cell(n):
+            cell_rows[n] = cell_bank.tile([P, BLOCKS, P], F32, name="cell_rows")
+            turn_back(cell_rows[n], cell_t[n])
+
+        def turn_sig_o(n):
+            sig_o_rows[n] = turn_pool.tile([P, BLOCKS, P], F32, name="sig_o_rows", tag="turned")
+            turn_back(sig_o_rows[n], gate[n, O_GATE])
+
+        def copy_cell(n):
+            r, m = divmod(n, CHUNKS)
+            cell[n] = result_pool.tile([P, BLOCKS, P], F32, name="cell")
+            nc.vector.tensor_copy(out=cell[n][:], in_=cell_rows[n][:])
+            nc.sync.dma_start(out=out_view[0, r, m], in_=cell[n][:])
+
+        def tanh_cell(n):
+            tanh_c[n] = cell_pool.tile([P, BLOCKS, P], F32, name="tanh_c")
+            nc.scalar.activation(out=tanh_c[n][:], in_=cell[n][:], func=ACT.Tanh)
+
+        def hidden(n):
+            r, m = divmod(n, CHUNKS)
+            hidden_rows = result_pool.tile([P, BLOCKS, P], F32, name="hidden_rows")
+            nc.vector.tensor_tensor(
+                out=hidden_rows[:], in0=tanh_c[n][:], in1=sig_o_rows[n][:], op=ALU.mult
+            )
+            nc.sync.dma_start(out=out_view[1, r, m], in_=hidden_rows[:])
+
+
+        load_biases()
+        load_unit(0)
+        load_unit(1)
+        load_weights(0)
+        load_weights(1)
+        load_unit(2)
+        load_weights(2)
+        load_unit(3)
+        load_weights(3)
+
+        nc.vector.memset(zero[:], 0.0)
+        nc.scalar.activation(out=half[:], in_=zero[:], func=ACT.Sigmoid)
+
+        for q in range(FIRST_UNITS):
+            add_z(q)
+            z_turned[q] = turn(z_sum[q])
+        nc.vector.tensor_copy(out=bias_rows_f32[:], in_=bias_rows[:])
+        bias_turned = cell_bank.tile([P, BLOCKS, P], F32, name="bias_turned", tag="cell_rows")
+        nc.tensor.transpose(bias_turned[:, 0, :], bias_rows_f32[:], ident[:])
+        for q in range(FIRST_UNITS):
+            z_grouped[q] = group(z_turned[q], prep, nc.vector.tensor_copy)
+        nc.vector.tensor_copy(out=bias[:], in_=bias_turned[:, 0, 0 : GATES * CHUNKS])
+        for m in range(FIRST_CHUNKS):
+            turn_weights(m)
+            group_weights(m, nc.scalar.copy)
+        for q in range(FIRST_UNITS):
+            quantise_z(q)
+        quantise_weights(0)
+        multiply(0)
+        quantise_weights(1)
+
+
+        for n in range(2 * FIRST_UNITS - LEAD, STEPS + LAST_LAG):
+            q, odd = divmod(n + LEAD, 2)
+
+            if 0 <= n - 1 < STEPS:
+                add_cell(n - 1)
+            if not odd and FIRST_UNITS <= q - 1 < Z_UNITS:
+                quantise_z(q - 1)
+            if not odd and q < Z_UNITS:
+                add_z(q)
+            if 0 <= n - 2 < STEPS:
+                copy_cell(n - 2)
+            if 0 <= n - LAST_LAG < STEPS:
+                hidden(n - LAST_LAG)
+            if odd and q < Z_UNITS:
+                z_grouped[q] = group(z_turned[q], prep, nc.vector.tensor_copy)
+            if FIRST_CHUNKS <= n + 2 < CHUNKS:
+                group_weights(n + 2, nc.vector.tensor_copy)
+                quantise_weights(n + 2)
+
+            if 0 <= n < STEPS:
+                activate(n, I_GATE)
+                activate(n, G_GATE)
+                multiply_gates(n)
+                activate(n, F_GATE)
+            if 0 <= n - 3 < STEPS:
+                tanh_cell(n - 3)
+            if 0 <= n < STEPS:
+                activate(n, O_GATE)
+
+            if 1 <= n + 1 < STEPS:
+                multiply(n + 1)
+            if 0 <= n - 1 < STEPS:
+                turn_cell(n - 1)
+            if 0 <= n - 3 < STEPS:
+                turn_sig_o(n - 3)
+            if not odd and q < Z_UNITS:
+                z_turned[q] = turn(z_sum[q])
+            if FIRST_CHUNKS <= n + 3 < CHUNKS:
+                turn_weights(n + 3)

@@ -30,10 +30,12 @@ PAIRS = BLOCKS // UNIT
 GATE_UNITS = GATES // UNIT
 Z_UNITS = B // (UNIT * P)
 FIRST_UNITS = PAIRS
-FIRST_CHUNKS = 2
-LEAD = 6
+FIRST_CHUNKS = 3
+WARM_UPS = 5
+LEAD = 5
 LOADS_AHEAD = 4
 LAST_LAG = 4
+FIRST_SUMMED = STEPS - 2
 
 FLOPS = 2 * B * H * GATES * H
 
@@ -115,31 +117,28 @@ def tile_lstmcell_pa_t_kernel(
             nc.vector.quantize_mx(out=codes.bitcast(FP8X4), scales=scales, in_=grouped[:])
 
 
-        def load_weights(m):
-            for g in range(GATES):
+        def load_weights(m, v):
+            for g in range(v * UNIT, (v + 1) * UNIT):
                 nc.sync.dma_start(out=w_raw[:, m, g, :], in_=weights[g][m * P : (m + 1) * P, :])
 
-        def turn_weights(m):
-            w_turned[m] = [
-                turn(w_raw[:, m, v * UNIT : (v + 1) * UNIT, :]) for v in range(GATE_UNITS)
-            ]
+        def turn_weights(m, v):
+            w_turned[m, v] = turn(w_raw[:, m, v * UNIT : (v + 1) * UNIT, :])
 
-        def group_weights(m, copy):
-            w_grouped[m] = [group(turned, w_prep, copy) for turned in w_turned[m]]
+        def group_weights(m, v, copy):
+            w_grouped[m, v] = group(w_turned[m, v], w_prep, copy)
 
-        def quantise_weights(m):
-            for v in range(GATE_UNITS):
-                gates_of_unit = slice(v * UNIT, (v + 1) * UNIT)
-                quantise(
-                    w_grouped[m][v],
-                    w_codes[:, m, gates_of_unit, :].rearrange("p g o -> p (g o)"),
-                    w_scales[:, m, gates_of_unit, :].rearrange("p g o -> p (g o)"),
-                )
+        def quantise_weights(m, v):
+            gates_of_unit = slice(v * UNIT, (v + 1) * UNIT)
+            quantise(
+                w_grouped[m, v],
+                w_codes[:, m, gates_of_unit, :].rearrange("p g o -> p (g o)"),
+                w_scales[:, m, gates_of_unit, :].rearrange("p g o -> p (g o)"),
+            )
 
         def load_biases():
             nc.vector.memset(bias_rows[:], 0.0)
             for g in range(GATES):
-                nc.scalar.dma_start(
+                nc.sync.dma_start(
                     out=bias_rows[g * CHUNKS : (g + 1) * CHUNKS, :],
                     in_=biases[g].rearrange("(m c) -> m c", c=P),
                 )
@@ -167,9 +166,9 @@ def tile_lstmcell_pa_t_kernel(
             quantise(z_grouped[q], z_codes[r][:, columns], z_scales[r][:, columns])
 
 
-        def multiply(n):
+        def multiply(n, gates=range(GATES)):
             r, m = divmod(n, CHUNKS)
-            for g in range(GATES):
+            for g in gates:
                 acc[n, g] = acc_pool.tile([P, ROUND], F32, name="acc")
                 nc.tensor.matmul_mx(
                     out=acc[n, g][:],
@@ -192,9 +191,9 @@ def tile_lstmcell_pa_t_kernel(
                 scale=1.0,
             )
 
-        def multiply_gates(n):
+        def multiply_gates(n, multiplier):
             product[n] = cell_pool.tile([P, ROUND], F32, name="product")
-            nc.gpsimd.tensor_tensor(
+            multiplier.tensor_tensor(
                 out=product[n][:], in0=gate[n, I_GATE][:], in1=gate[n, G_GATE][:], op=ALU.mult
             )
 
@@ -204,17 +203,29 @@ def tile_lstmcell_pa_t_kernel(
                 out=cell_t[n][:], in0=gate[n, F_GATE][:], in1=product[n][:], op=ALU.add
             )
 
-        def turn_back(rows, source):
+        def turn_back(rows, sources):
             for s in range(BLOCKS):
-                nc.tensor.transpose(rows[:, s, :], source[:, s * P : (s + 1) * P], ident[:])
+                for i, source in enumerate(sources):
+                    nc.tensor.matmul(
+                        out=rows[:, s, :],
+                        lhsT=source[:, s * P : (s + 1) * P],
+                        rhs=ident[:],
+                        start=i == 0,
+                        stop=i == len(sources) - 1,
+                        is_transpose=True,
+                    )
 
         def turn_cell(n):
-            cell_rows[n] = cell_bank.tile([P, BLOCKS, P], F32, name="cell_rows")
-            turn_back(cell_rows[n], cell_t[n])
+            if n < FIRST_SUMMED:
+                cell_rows[n] = cell_bank.tile([P, BLOCKS, P], F32, name="cell_rows")
+                turn_back(cell_rows[n], [cell_t[n]])
+            else:
+                cell_rows[n] = acc_pool.tile([P, BLOCKS, P], F32, name="last_rows", tag="acc")
+                turn_back(cell_rows[n], [gate[n, F_GATE], product[n]])
 
         def turn_sig_o(n):
             sig_o_rows[n] = turn_pool.tile([P, BLOCKS, P], F32, name="sig_o_rows", tag="turned")
-            turn_back(sig_o_rows[n], gate[n, O_GATE])
+            turn_back(sig_o_rows[n], [gate[n, O_GATE]])
 
         def copy_cell(n):
             r, m = divmod(n, CHUNKS)
@@ -229,80 +240,132 @@ def tile_lstmcell_pa_t_kernel(
         def hidden(n):
             r, m = divmod(n, CHUNKS)
             hidden_rows = result_pool.tile([P, BLOCKS, P], F32, name="hidden_rows")
-            nc.vector.tensor_tensor(
-                out=hidden_rows[:], in0=tanh_c[n][:], in1=sig_o_rows[n][:], op=ALU.mult
-            )
-            nc.sync.dma_start(out=out_view[1, r, m], in_=hidden_rows[:])
+            parts = 2 if n == STEPS - 1 else 1
+            for part in range(parts):
+                rows = slice(part * BLOCKS // parts, (part + 1) * BLOCKS // parts)
+                nc.vector.tensor_tensor(
+                    out=hidden_rows[:, rows, :],
+                    in0=tanh_c[n][:, rows, :],
+                    in1=sig_o_rows[n][:, rows, :],
+                    op=ALU.mult,
+                )
+                nc.sync.dma_start(out=out_view[1, r, m, :, rows, :], in_=hidden_rows[:, rows, :])
 
 
-        load_biases()
         load_unit(0)
+        load_weights(0, 0)
         load_unit(1)
-        load_weights(0)
-        load_weights(1)
+        load_weights(0, 1)
+        load_biases()
+        for m in range(1, FIRST_CHUNKS):
+            for v in range(GATE_UNITS):
+                load_weights(m, v)
         load_unit(2)
-        load_weights(2)
+        for m in range(FIRST_CHUNKS, CHUNKS):
+            for v in range(GATE_UNITS):
+                load_weights(m, v)
         load_unit(3)
-        load_weights(3)
 
         nc.vector.memset(zero[:], 0.0)
         nc.scalar.activation(out=half[:], in_=zero[:], func=ACT.Sigmoid)
 
-        for q in range(FIRST_UNITS):
-            add_z(q)
-            z_turned[q] = turn(z_sum[q])
+        warm = cell_bank.tile([P, BLOCKS, P], F32, name="warm", tag="cell_rows")
+        for i in range(WARM_UPS):
+            nc.tensor.matmul(out=warm[:, 0, :], lhsT=ident[:], rhs=ident[:], start=True, stop=True)
+
+        i_and_g, f_and_o = [range(v * UNIT, (v + 1) * UNIT) for v in range(GATE_UNITS)]
+        add_z(0)
+        z_turned[0] = turn(z_sum[0])
+        z_grouped[0] = group(z_turned[0], prep, nc.scalar.copy)
+        turn_weights(0, 0)
+        add_z(1)
+        z_turned[1] = turn(z_sum[1])
+        group_weights(0, 0, nc.vector.tensor_copy)
+        z_grouped[1] = group(z_turned[1], prep, nc.scalar.copy)
+        quantise_z(0)
+        quantise_weights(0, 0)
+        turn_weights(0, 1)
+        group_weights(0, 1, nc.scalar.copy)
         nc.vector.tensor_copy(out=bias_rows_f32[:], in_=bias_rows[:])
         bias_turned = cell_bank.tile([P, BLOCKS, P], F32, name="bias_turned", tag="cell_rows")
         nc.tensor.transpose(bias_turned[:, 0, :], bias_rows_f32[:], ident[:])
-        for q in range(FIRST_UNITS):
-            z_grouped[q] = group(z_turned[q], prep, nc.vector.tensor_copy)
+        quantise_z(1)
         nc.vector.tensor_copy(out=bias[:], in_=bias_turned[:, 0, 0 : GATES * CHUNKS])
-        for m in range(FIRST_CHUNKS):
-            turn_weights(m)
-            group_weights(m, nc.scalar.copy)
-        for q in range(FIRST_UNITS):
-            quantise_z(q)
-        quantise_weights(0)
-        multiply(0)
-        quantise_weights(1)
+        turn_weights(1, 0)
+        multiply(0, i_and_g)
+        quantise_weights(0, 1)
+        multiply(0, f_and_o)
+        turn_weights(1, 1)
+        for m in range(1, FIRST_CHUNKS):
+            for v in range(GATE_UNITS):
+                group_weights(m, v, nc.vector.tensor_copy)
+                if m + 1 < FIRST_CHUNKS:
+                    turn_weights(m + 1, v)
+            for v in range(GATE_UNITS):
+                quantise_weights(m, v)
+            if m == 1:
+                multiply(1)
 
 
-        for n in range(2 * FIRST_UNITS - LEAD, STEPS + LAST_LAG):
-            q, odd = divmod(n + LEAD, 2)
+        add_turn = {q: 1 if q < 2 * PAIRS else 2 * q - LEAD for q in range(FIRST_UNITS, Z_UNITS)}
 
-            if 0 <= n - 1 < STEPS:
+        for n in range(STEPS):
+            added = [q for q in add_turn if add_turn[q] == n]
+            grouped = [q for q in add_turn if add_turn[q] == n - 1]
+            quantised = [q for q in add_turn if add_turn[q] == n - 2]
+
+            for q in quantised:
+                quantise_z(q)
+            if 0 <= n - 1 < FIRST_SUMMED:
                 add_cell(n - 1)
-            if not odd and FIRST_UNITS <= q - 1 < Z_UNITS:
-                quantise_z(q - 1)
-            if not odd and q < Z_UNITS:
+            for q in added:
                 add_z(q)
-            if 0 <= n - 2 < STEPS:
+            if 0 <= n - 2:
                 copy_cell(n - 2)
-            if 0 <= n - LAST_LAG < STEPS:
-                hidden(n - LAST_LAG)
-            if odd and q < Z_UNITS:
-                z_grouped[q] = group(z_turned[q], prep, nc.vector.tensor_copy)
             if FIRST_CHUNKS <= n + 2 < CHUNKS:
-                group_weights(n + 2, nc.vector.tensor_copy)
-                quantise_weights(n + 2)
+                for v in range(GATE_UNITS):
+                    group_weights(n + 2, v, nc.vector.tensor_copy)
+                for v in range(GATE_UNITS):
+                    quantise_weights(n + 2, v)
+            if 0 <= n - LAST_LAG:
+                hidden(n - LAST_LAG)
+            for q in grouped:
+                z_grouped[q] = group(z_turned[q], prep, nc.vector.tensor_copy)
 
-            if 0 <= n < STEPS:
-                activate(n, I_GATE)
-                activate(n, G_GATE)
-                multiply_gates(n)
-                activate(n, F_GATE)
-            if 0 <= n - 3 < STEPS:
+            activate(n, I_GATE)
+            activate(n, G_GATE)
+            if n < STEPS - 1:
+                multiply_gates(n, nc.gpsimd)
+            activate(n, F_GATE)
+            if 0 <= n - 3:
                 tanh_cell(n - 3)
-            if 0 <= n < STEPS:
-                activate(n, O_GATE)
+            activate(n, O_GATE)
 
-            if 1 <= n + 1 < STEPS:
+            if 2 <= n + 1 < STEPS:
                 multiply(n + 1)
-            if 0 <= n - 1 < STEPS:
+            if 0 <= n - 1:
                 turn_cell(n - 1)
-            if 0 <= n - 3 < STEPS:
+            if 0 <= n - 3:
                 turn_sig_o(n - 3)
-            if not odd and q < Z_UNITS:
-                z_turned[q] = turn(z_sum[q])
             if FIRST_CHUNKS <= n + 3 < CHUNKS:
-                turn_weights(n + 3)
+                for v in range(GATE_UNITS):
+                    turn_weights(n + 3, v)
+            for q in added:
+                z_turned[q] = turn(z_sum[q])
+
+
+        last = STEPS - 1
+        copy_cell(last - 1)
+        multiply_gates(last, nc.vector)
+        turn_sig_o(last - 2)
+        turn_cell(last)
+        turn_sig_o(last - 1)
+        tanh_cell(last - 2)
+        hidden(last - 3)
+        tanh_cell(last - 1)
+        copy_cell(last)
+        hidden(last - 2)
+        turn_sig_o(last)
+        tanh_cell(last)
+        hidden(last - 1)
+        hidden(last)

@@ -25,14 +25,13 @@ BLOCKS = ROUND // P
 STEPS = (B // ROUND) * CHUNKS
 PARITIES = 2
 UNIT = 2
-UNIT_COLS = UNIT * P
 PAIRS = BLOCKS // UNIT
 GATE_UNITS = GATES // UNIT
-Z_UNITS = B // (UNIT * P)
-FIRST_UNITS = PAIRS
+Z_BLOCKS = B // P
+Z_UNITS = Z_BLOCKS // UNIT
 FIRST_CHUNKS = 3
 WARM_UPS = 5
-LEAD = 5
+LEAD = 6
 LOADS_AHEAD = 4
 LAST_LAG = 4
 FIRST_SUMMED = STEPS - 2
@@ -97,18 +96,18 @@ def tile_lstmcell_pa_t_kernel(
         tanh_c = {}
 
 
-        def turn(source):
-            turned = turn_pool.tile([P, UNIT, PARITIES, P], F32, name="unit_turned", tag="turned")
-            for t in range(UNIT):
+        def turn(source, count):
+            turned = turn_pool.tile([P, count, PARITIES, P], F32, name="unit_turned", tag="turned")
+            for t in range(count):
                 words = source[:, t, :].bitcast(F32)
                 for u in range(PARITIES):
                     nc.tensor.transpose(turned[:, t, u, :], words[:, u :: PARITIES], ident[:])
             return turned
 
-        def group(turned, pool, copy):
-            grouped = pool.tile([P, UNIT * H], BF16, name="grouped", align_bytes=64)
+        def group(turned, count, pool, copy):
+            grouped = pool.tile([P, count * H], BF16, name="grouped", align_bytes=64)
             copy(
-                out=grouped[:].bitcast(F32).rearrange("p (t c u) -> p t c u", t=UNIT, u=PARITIES),
+                out=grouped[:].bitcast(F32).rearrange("p (t c u) -> p t c u", t=count, u=PARITIES),
                 in_=turned[:].rearrange("p t u c -> p t c u"),
             )
             return grouped
@@ -122,10 +121,10 @@ def tile_lstmcell_pa_t_kernel(
                 nc.sync.dma_start(out=w_raw[:, m, g, :], in_=weights[g][m * P : (m + 1) * P, :])
 
         def turn_weights(m, v):
-            w_turned[m, v] = turn(w_raw[:, m, v * UNIT : (v + 1) * UNIT, :])
+            w_turned[m, v] = turn(w_raw[:, m, v * UNIT : (v + 1) * UNIT, :], UNIT)
 
         def group_weights(m, v, copy):
-            w_grouped[m, v] = group(w_turned[m, v], w_prep, copy)
+            w_grouped[m, v] = group(w_turned[m, v], UNIT, w_prep, copy)
 
         def quantise_weights(m, v):
             gates_of_unit = slice(v * UNIT, (v + 1) * UNIT)
@@ -151,19 +150,31 @@ def tile_lstmcell_pa_t_kernel(
             h_raw[q] = loads.tile([P, UNIT, H], BF16, name="h_raw")
             nc.sync.dma_start(out=h_raw[q][:], in_=h_view[r, a])
 
-        def add_z(q):
-            z_sum[q] = prep.tile([P, UNIT, H], BF16, name="z_sum")
-            nc.vector.tensor_tensor(out=z_sum[q][:], in0=x_raw[q][:], in1=h_raw[q][:], op=ALU.add)
-            if q + LOADS_AHEAD < Z_UNITS:
+        def add_z(b, count):
+            q, t = divmod(b, UNIT)
+            z_sum[b] = prep.tile([P, count, H], BF16, name="z_sum")
+            nc.vector.tensor_tensor(
+                out=z_sum[b][:],
+                in0=x_raw[q][:, t : t + count, :],
+                in1=h_raw[q][:, t : t + count, :],
+                op=ALU.add,
+            )
+            if t + count == UNIT and q + LOADS_AHEAD < Z_UNITS:
                 load_unit(q + LOADS_AHEAD)
 
-        def quantise_z(q):
-            r, a = divmod(q, PAIRS)
-            if a == 0:
+        def turn_z(b, count):
+            z_turned[b] = turn(z_sum[b], count)
+
+        def group_z(b, count, copy):
+            z_grouped[b] = group(z_turned[b], count, prep, copy)
+
+        def quantise_z(b, count):
+            r, s = divmod(b, BLOCKS)
+            if s == 0:
                 z_codes[r] = prep.tile([P, ROUND], U32, name="z_codes", align_bytes=64)
                 z_scales[r] = prep.tile([P, ROUND], U8, name="z_scales", align_bytes=64)
-            columns = slice(a * UNIT_COLS, (a + 1) * UNIT_COLS)
-            quantise(z_grouped[q], z_codes[r][:, columns], z_scales[r][:, columns])
+            columns = slice(s * P, (s + count) * P)
+            quantise(z_grouped[b], z_codes[r][:, columns], z_scales[r][:, columns])
 
 
         def multiply(n, gates=range(GATES)):
@@ -274,22 +285,22 @@ def tile_lstmcell_pa_t_kernel(
             nc.tensor.matmul(out=warm[:, 0, :], lhsT=ident[:], rhs=ident[:], start=True, stop=True)
 
         i_and_g, f_and_o = [range(v * UNIT, (v + 1) * UNIT) for v in range(GATE_UNITS)]
-        add_z(0)
-        z_turned[0] = turn(z_sum[0])
-        z_grouped[0] = group(z_turned[0], prep, nc.scalar.copy)
+        add_z(0, UNIT)
+        turn_z(0, UNIT)
+        group_z(0, UNIT, nc.scalar.copy)
         turn_weights(0, 0)
-        add_z(1)
-        z_turned[1] = turn(z_sum[1])
+        add_z(UNIT, UNIT)
+        turn_z(UNIT, UNIT)
         group_weights(0, 0, nc.vector.tensor_copy)
-        z_grouped[1] = group(z_turned[1], prep, nc.scalar.copy)
-        quantise_z(0)
+        group_z(UNIT, UNIT, nc.scalar.copy)
+        quantise_z(0, UNIT)
         quantise_weights(0, 0)
         turn_weights(0, 1)
         group_weights(0, 1, nc.scalar.copy)
         nc.vector.tensor_copy(out=bias_rows_f32[:], in_=bias_rows[:])
         bias_turned = cell_bank.tile([P, BLOCKS, P], F32, name="bias_turned", tag="cell_rows")
         nc.tensor.transpose(bias_turned[:, 0, :], bias_rows_f32[:], ident[:])
-        quantise_z(1)
+        quantise_z(UNIT, UNIT)
         nc.vector.tensor_copy(out=bias[:], in_=bias_turned[:, 0, 0 : GATES * CHUNKS])
         turn_weights(1, 0)
         multiply(0, i_and_g)
@@ -307,19 +318,20 @@ def tile_lstmcell_pa_t_kernel(
                 multiply(1)
 
 
-        add_turn = {q: 1 if q < 2 * PAIRS else 2 * q - LEAD for q in range(FIRST_UNITS, Z_UNITS)}
+        jobs = [(b, UNIT, 1) for b in range(BLOCKS, 2 * BLOCKS, UNIT)]
+        jobs += [(b, 1, b - LEAD) for b in range(2 * BLOCKS, Z_BLOCKS)]
 
         for n in range(STEPS):
-            added = [q for q in add_turn if add_turn[q] == n]
-            grouped = [q for q in add_turn if add_turn[q] == n - 1]
-            quantised = [q for q in add_turn if add_turn[q] == n - 2]
+            added, grouped, quantised = [
+                [(b, count) for b, count, added_in in jobs if added_in == n - age] for age in range(3)
+            ]
 
-            for q in quantised:
-                quantise_z(q)
+            for b, count in quantised:
+                quantise_z(b, count)
             if 0 <= n - 1 < FIRST_SUMMED:
                 add_cell(n - 1)
-            for q in added:
-                add_z(q)
+            for b, count in added:
+                add_z(b, count)
             if 0 <= n - 2:
                 copy_cell(n - 2)
             if FIRST_CHUNKS <= n + 2 < CHUNKS:
@@ -329,8 +341,8 @@ def tile_lstmcell_pa_t_kernel(
                     quantise_weights(n + 2, v)
             if 0 <= n - LAST_LAG:
                 hidden(n - LAST_LAG)
-            for q in grouped:
-                z_grouped[q] = group(z_turned[q], prep, nc.vector.tensor_copy)
+            for b, count in grouped:
+                group_z(b, count, nc.vector.tensor_copy)
 
             activate(n, I_GATE)
             activate(n, G_GATE)
@@ -342,21 +354,25 @@ def tile_lstmcell_pa_t_kernel(
             activate(n, O_GATE)
 
             if 2 <= n + 1 < STEPS:
-                multiply(n + 1)
+                multiply(n + 1, i_and_g)
+                if n + 1 < STEPS - 1:
+                    multiply(n + 1, f_and_o)
             if 0 <= n - 1:
                 turn_cell(n - 1)
             if 0 <= n - 3:
                 turn_sig_o(n - 3)
+            if n + 1 == STEPS - 1:
+                multiply(n + 1, f_and_o)
             if FIRST_CHUNKS <= n + 3 < CHUNKS:
                 for v in range(GATE_UNITS):
                     turn_weights(n + 3, v)
-            for q in added:
-                z_turned[q] = turn(z_sum[q])
+            for b, count in added:
+                turn_z(b, count)
 
 
         last = STEPS - 1
-        copy_cell(last - 1)
         multiply_gates(last, nc.vector)
+        copy_cell(last - 1)
         turn_sig_o(last - 2)
         turn_cell(last)
         turn_sig_o(last - 1)

@@ -373,15 +373,10 @@ def tile_lstmcell_pa_t_kernel(
         last = STEPS - 1
         multiply_gates(last, nc.vector)
         copy_cell(last - 1)
-        turn_sig_o(last - 2)
         turn_cell(last)
-        turn_sig_o(last - 1)
-        tanh_cell(last - 2)
         hidden(last - 3)
-        tanh_cell(last - 1)
         copy_cell(last)
-        hidden(last - 2)
-        turn_sig_o(last)
-        tanh_cell(last)
-        hidden(last - 1)
-        hidden(last)
+        for n in range(last - 2, STEPS):
+            turn_sig_o(n)
+            tanh_cell(n)
+            hidden(n)

@@ -30,7 +30,8 @@ GATE_UNITS = GATES // UNIT
 Z_BLOCKS = B // P
 Z_UNITS = Z_BLOCKS // UNIT
 FIRST_CHUNKS = 3
-WARM_UPS = 5
+FIRST_WARM_UPS = 6
+WARM_UPS = 2
 LEAD = 6
 LOADS_AHEAD = 4
 LAST_LAG = 4
@@ -96,8 +97,13 @@ def tile_lstmcell_pa_t_kernel(
         tanh_c = {}
 
 
-        def turn(source, count):
+        def warm_up(bank, count):
+            for i in range(count):
+                nc.tensor.matmul(out=bank, lhsT=ident[:], rhs=ident[:], start=True, stop=True)
+
+        def turn(source, count, warm_ups=0):
             turned = turn_pool.tile([P, count, PARITIES, P], F32, name="unit_turned", tag="turned")
+            warm_up(turned[:, 0, 0, :], warm_ups)
             for t in range(count):
                 words = source[:, t, :].bitcast(F32)
                 for u in range(PARITIES):
@@ -120,8 +126,8 @@ def tile_lstmcell_pa_t_kernel(
             for g in range(v * UNIT, (v + 1) * UNIT):
                 nc.sync.dma_start(out=w_raw[:, m, g, :], in_=weights[g][m * P : (m + 1) * P, :])
 
-        def turn_weights(m, v):
-            w_turned[m, v] = turn(w_raw[:, m, v * UNIT : (v + 1) * UNIT, :], UNIT)
+        def turn_weights(m, v, warm_ups=0):
+            w_turned[m, v] = turn(w_raw[:, m, v * UNIT : (v + 1) * UNIT, :], UNIT, warm_ups)
 
         def group_weights(m, v, copy):
             w_grouped[m, v] = group(w_turned[m, v], UNIT, w_prep, copy)
@@ -162,8 +168,8 @@ def tile_lstmcell_pa_t_kernel(
             if t + count == UNIT and q + LOADS_AHEAD < Z_UNITS:
                 load_unit(q + LOADS_AHEAD)
 
-        def turn_z(b, count):
-            z_turned[b] = turn(z_sum[b], count)
+        def turn_z(b, count, warm_ups=0):
+            z_turned[b] = turn(z_sum[b], count, warm_ups)
 
         def group_z(b, count, copy):
             z_grouped[b] = group(z_turned[b], count, prep, copy)
@@ -281,8 +287,7 @@ def tile_lstmcell_pa_t_kernel(
         nc.scalar.activation(out=half[:], in_=zero[:], func=ACT.Sigmoid)
 
         warm = cell_bank.tile([P, BLOCKS, P], F32, name="warm", tag="cell_rows")
-        for i in range(WARM_UPS):
-            nc.tensor.matmul(out=warm[:, 0, :], lhsT=ident[:], rhs=ident[:], start=True, stop=True)
+        warm_up(warm[:, 0, :], FIRST_WARM_UPS)
 
         i_and_g, f_and_o = [range(v * UNIT, (v + 1) * UNIT) for v in range(GATE_UNITS)]
         add_z(0, UNIT)
@@ -290,7 +295,7 @@ def tile_lstmcell_pa_t_kernel(
         group_z(0, UNIT, nc.scalar.copy)
         turn_weights(0, 0)
         add_z(UNIT, UNIT)
-        turn_z(UNIT, UNIT)
+        turn_z(UNIT, UNIT, WARM_UPS)
         group_weights(0, 0, nc.vector.tensor_copy)
         group_z(UNIT, UNIT, nc.scalar.copy)
         quantise_z(0, UNIT)
@@ -302,7 +307,7 @@ def tile_lstmcell_pa_t_kernel(
         nc.tensor.transpose(bias_turned[:, 0, :], bias_rows_f32[:], ident[:])
         quantise_z(UNIT, UNIT)
         nc.vector.tensor_copy(out=bias[:], in_=bias_turned[:, 0, 0 : GATES * CHUNKS])
-        turn_weights(1, 0)
+        turn_weights(1, 0, WARM_UPS - 1)
         multiply(0, i_and_g)
         quantise_weights(0, 1)
         multiply(0, f_and_o)

from contextlib import ExitStack

import concourse.mybir as mybir
from concourse.masks import make_identity

F32 = mybir.dt.float32
BF16 = mybir.dt.bfloat16
U32 = mybir.dt.uint32
U8 = mybir.dt.uint8
FP8X4 = mybir.dt.float8_e4m3fn_x4
ACT = mybir.ActivationFunctionType
ALU = mybir.AluOpType

B = 4096
H = 512
P = 128
GATES = 4
I_GATE = 0
G_GATE = 1
F_GATE = 2
O_GATE = 3
ROUND = 512
CHUNKS = H // P
BLOCKS = ROUND // P
STEPS = (B // ROUND) * CHUNKS
PARITIES = 2
UNIT = 2
PAIRS = BLOCKS // UNIT
GATE_UNITS = GATES // UNIT
Z_BLOCKS = B // P
Z_UNITS = Z_BLOCKS // UNIT
FIRST_CHUNKS = 3
FIRST_WARM_UPS = 6
WARM_UPS = 2
LEAD = 6
LOADS_AHEAD = 4
LAST_LAG = 4
FIRST_SUMMED = STEPS - 2

FLOPS = 2 * B * H * GATES * H


def tile_lstmcell_pa_t_kernel(
    tc, inputs, short_term_memory, Wf, b_f, Wi, b_i, Wg, b_g, Wo, b_o, out
):
    nc = tc.nc
    weights = [Wi, Wg, Wf, Wo]
    biases = [b_i, b_g, b_f, b_o]
    functions = [ACT.Sigmoid, ACT.Tanh, ACT.Sigmoid, ACT.Sigmoid]
    gate_names = ["sig_i", "tanh_g", "sig_f", "sig_o"]
    x_view = inputs.rearrange("(r p a t) k -> r a p t k", p=P, a=PAIRS, t=UNIT)
    h_view = short_term_memory.rearrange("(r p a t) k -> r a p t k", p=P, a=PAIRS, t=UNIT)
    out_view = out.rearrange("o (r p s) (m f) -> o r m p s f", p=P, s=BLOCKS, f=P)

    with ExitStack() as ctx:
        keep = ctx.enter_context(tc.tile_pool(name="keep", bufs=1))
        loads = ctx.enter_context(tc.tile_pool(name="loads", bufs=LOADS_AHEAD))
        prep = ctx.enter_context(tc.tile_pool(name="prep", bufs=3))
        w_prep = ctx.enter_context(tc.tile_pool(name="w_prep", bufs=FIRST_CHUNKS * GATE_UNITS))
        gate_pool = ctx.enter_context(tc.tile_pool(name="gates", bufs=LAST_LAG + 1))
        cell_pool = ctx.enter_context(tc.tile_pool(name="cells", bufs=3))
        result_pool = ctx.enter_context(tc.tile_pool(name="results", bufs=4))
        acc_pool = ctx.enter_context(tc.psum_pool(name="acc", bufs=GATES))
        cell_bank = ctx.enter_context(tc.psum_pool(name="cell_bank", bufs=1))
        turn_pool = ctx.enter_context(tc.psum_pool(name="turned", bufs=3))

        ident = keep.tile([P, P], F32, name="ident")
        make_identity(nc, ident[:])

        ctx.enter_context(tc.manual_schedule())

        w_raw = keep.tile([P, CHUNKS, GATES, H], BF16, name="w_raw")
        w_codes = keep.tile([P, CHUNKS, GATES, P], U32, name="w_codes", align_bytes=64)
        w_scales = keep.tile([P, CHUNKS, GATES, P], U8, name="w_scales", align_bytes=64)
        bias_rows = keep.tile([P, P], BF16, name="bias_rows")
        bias_rows_f32 = keep.tile([P, P], F32, name="bias_rows_f32")
        bias = keep.tile([P, GATES * CHUNKS], F32, name="bias")
        zero = keep.tile([P, 1], F32, name="zero")
        half = keep.tile([P, 1], F32, name="half")

        w_turned = {}
        w_grouped = {}
        x_raw = {}
        h_raw = {}
        z_sum = {}
        z_turned = {}
        z_grouped = {}
        z_codes = {}
        z_scales = {}
        acc = {}
        gate = {}
        product = {}
        cell_t = {}
        cell_rows = {}
        sig_o_rows = {}
        cell = {}
        tanh_c = {}


        def warm_up(bank, count):
            for i in range(count):
                nc.tensor.matmul(out=bank, lhsT=ident[:], rhs=ident[:], start=True, stop=True)

        def turn(source, count, warm_ups=0):
            turned = turn_pool.tile([P, count, PARITIES, P], F32, name="unit_turned", tag="turned")
            warm_up(turned[:, 0, 0, :], warm_ups)
            for t in range(count):
                words = source[:, t, :].bitcast(F32)
                for u in range(PARITIES):
                    nc.tensor.transpose(turned[:, t, u, :], words[:, u :: PARITIES], ident[:])
            return turned

        def group(turned, count, pool, copy):
            grouped = pool.tile([P, count * H], BF16, name="grouped", align_bytes=64)
            copy(
                out=grouped[:].bitcast(F32).rearrange("p (t c u) -> p t c u", t=count, u=PARITIES),
                in_=turned[:].rearrange("p t u c -> p t c u"),
            )
            return grouped

        def quantise(grouped, codes, scales):
            nc.vector.quantize_mx(out=codes.bitcast(FP8X4), scales=scales, in_=grouped[:])


        def load_weights(m, v):
            for g in range(v * UNIT, (v + 1) * UNIT):
                nc.sync.dma_start(out=w_raw[:, m, g, :], in_=weights[g][m * P : (m + 1) * P, :])

        def turn_weights(m, v, warm_ups=0):
            w_turned[m, v] = turn(w_raw[:, m, v * UNIT : (v + 1) * UNIT, :], UNIT, warm_ups)

        def group_weights(m, v, copy):
            w_grouped[m, v] = group(w_turned[m, v], UNIT, w_prep, copy)

        def quantise_weights(m, v):
            gates_of_unit = slice(v * UNIT, (v + 1) * UNIT)
            quantise(
                w_grouped[m, v],
                w_codes[:, m, gates_of_unit, :].rearrange("p g o -> p (g o)"),
                w_scales[:, m, gates_of_unit, :].rearrange("p g o -> p (g o)"),
            )

        def load_biases():
            nc.vector.memset(bias_rows[:], 0.0)
            for g in range(GATES):
                nc.sync.dma_start(
                    out=bias_rows[g * CHUNKS : (g + 1) * CHUNKS, :],
                    in_=biases[g].rearrange("(m c) -> m c", c=P),
                )


        def load_unit(q):
            r, a = divmod(q, PAIRS)
            x_raw[q] = loads.tile([P, UNIT, H], BF16, name="x_raw")
            nc.sync.dma_start(out=x_raw[q][:], in_=x_view[r, a])
            h_raw[q] = loads.tile([P, UNIT, H], BF16, name="h_raw")
            nc.sync.dma_start(out=h_raw[q][:], in_=h_view[r, a])

        def add_z(b, count):
            q, t = divmod(b, UNIT)
            z_sum[b] = prep.tile([P, count, H], BF16, name="z_sum")
            nc.vector.tensor_tensor(
                out=z_sum[b][:],
                in0=x_raw[q][:, t : t + count, :],
                in1=h_raw[q][:, t : t + count, :],
                op=ALU.add,
            )
            if t + count == UNIT and q + LOADS_AHEAD < Z_UNITS:
                load_unit(q + LOADS_AHEAD)

        def turn_z(b, count, warm_ups=0):
            z_turned[b] = turn(z_sum[b], count, warm_ups)

        def group_z(b, count, copy):
            z_grouped[b] = group(z_turned[b], count, prep, copy)

        def quantise_z(b, count):
            r, s = divmod(b, BLOCKS)
            if s == 0:
                z_codes[r] = prep.tile([P, ROUND], U32, name="z_codes", align_bytes=64)
                z_scales[r] = prep.tile([P, ROUND], U8, name="z_scales", align_bytes=64)
            columns = slice(s * P, (s + count) * P)
            quantise(z_grouped[b], z_codes[r][:, columns], z_scales[r][:, columns])


        def multiply(n, gates=range(GATES)):
            r, m = divmod(n, CHUNKS)
            for g in gates:
                acc[n, g] = acc_pool.tile([P, ROUND], F32, name="acc")
                nc.tensor.matmul_mx(
                    out=acc[n, g][:],
                    lhsT=w_codes[:, m, g, :].bitcast(FP8X4),
                    lhsT_scale=w_scales[:, m, g, :],
                    rhs=z_codes[r][:].bitcast(FP8X4),
                    rhs_scale=z_scales[r][:],
                    start=True,
                    stop=True,
                )

        def activate(n, g):
            gate[n, g] = gate_pool.tile([P, ROUND], F32, name=gate_names[g])
            column = g * CHUNKS + n % CHUNKS
            nc.scalar.activation(
                out=gate[n, g][:],
                in_=acc[n, g][:],
                func=functions[g],
                bias=bias[:, column : column + 1],
                scale=1.0,
            )

        def multiply_gates(n, multiplier):
            product[n] = cell_pool.tile([P, ROUND], F32, name="product")
            multiplier.tensor_tensor(
                out=product[n][:], in0=gate[n, I_GATE][:], in1=gate[n, G_GATE][:], op=ALU.mult
            )

        def add_cell(n):
            cell_t[n] = cell_pool.tile([P, ROUND], F32, name="cell_t")
            nc.vector.tensor_tensor(
                out=cell_t[n][:], in0=gate[n, F_GATE][:], in1=product[n][:], op=ALU.add
            )

        def turn_back(rows, sources):
            for s in range(BLOCKS):
                for i, source in enumerate(sources):
                    nc.tensor.matmul(
                        out=rows[:, s, :],
                        lhsT=source[:, s * P : (s + 1) * P],
                        rhs=ident[:],
                        start=i == 0,
                        stop=i == len(sources) - 1,
                        is_transpose=True,
                    )

        def turn_cell(n):
            if n < FIRST_SUMMED:
                cell_rows[n] = cell_bank.tile([P, BLOCKS, P], F32, name="cell_rows")
                turn_back(cell_rows[n], [cell_t[n]])
            else:
                cell_rows[n] = acc_pool.tile([P, BLOCKS, P], F32, name="last_rows", tag="acc")
                turn_back(cell_rows[n], [gate[n, F_GATE], product[n]])

        def turn_sig_o(n):
            sig_o_rows[n] = turn_pool.tile([P, BLOCKS, P], F32, name="sig_o_rows", tag="turned")
            turn_back(sig_o_rows[n], [gate[n, O_GATE]])

        def copy_cell(n):
            r, m = divmod(n, CHUNKS)
            cell[n] = result_pool.tile([P, BLOCKS, P], F32, name="cell")
            nc.vector.tensor_copy(out=cell[n][:], in_=cell_rows[n][:])
            nc.sync.dma_start(out=out_view[0, r, m], in_=cell[n][:])

        def tanh_cell(n):
            tanh_c[n] = cell_pool.tile([P, BLOCKS, P], F32, name="tanh_c")
            nc.scalar.activation(out=tanh_c[n][:], in_=cell[n][:], func=ACT.Tanh)

        def hidden(n):
            r, m = divmod(n, CHUNKS)
            hidden_rows = result_pool.tile([P, BLOCKS, P], F32, name="hidden_rows")
            parts = 2 if n == STEPS - 1 else 1
            for part in range(parts):
                rows = slice(part * BLOCKS // parts, (part + 1) * BLOCKS // parts)
                nc.vector.tensor_tensor(
                    out=hidden_rows[:, rows, :],
                    in0=tanh_c[n][:, rows, :],
                    in1=sig_o_rows[n][:, rows, :],
                    op=ALU.mult,
                )
                nc.sync.dma_start(out=out_view[1, r, m, :, rows, :], in_=hidden_rows[:, rows, :])


        load_unit(0)
        load_weights(0, 0)
        load_unit(1)
        load_weights(0, 1)
        load_biases()
        for m in range(1, FIRST_CHUNKS):
            for v in range(GATE_UNITS):
                load_weights(m, v)
        load_unit(2)
        for m in range(FIRST_CHUNKS, CHUNKS):
            for v in range(GATE_UNITS):
                load_weights(m, v)
        load_unit(3)

        nc.vector.memset(zero[:], 0.0)
        nc.scalar.activation(out=half[:], in_=zero[:], func=ACT.Sigmoid)

        warm = cell_bank.tile([P, BLOCKS, P], F32, name="warm", tag="cell_rows")
        warm_up(warm[:, 0, :], FIRST_WARM_UPS)

        i_and_g, f_and_o = [range(v * UNIT, (v + 1) * UNIT) for v in range(GATE_UNITS)]
        add_z(0, UNIT)
        turn_z(0, UNIT)
        group_z(0, UNIT, nc.scalar.copy)
        turn_weights(0, 0)
        add_z(UNIT, UNIT)
        turn_z(UNIT, UNIT, WARM_UPS)
        group_weights(0, 0, nc.vector.tensor_copy)
        group_z(UNIT, UNIT, nc.scalar.copy)
        quantise_z(0, UNIT)
        quantise_weights(0, 0)
        turn_weights(0, 1)
        group_weights(0, 1, nc.scalar.copy)
        nc.vector.tensor_copy(out=bias_rows_f32[:], in_=bias_rows[:])
        bias_turned = cell_bank.tile([P, BLOCKS, P], F32, name="bias_turned", tag="cell_rows")
        nc.tensor.transpose(bias_turned[:, 0, :], bias_rows_f32[:], ident[:])
        quantise_z(UNIT, UNIT)
        nc.vector.tensor_copy(out=bias[:], in_=bias_turned[:, 0, 0 : GATES * CHUNKS])
        turn_weights(1, 0, WARM_UPS - 1)
        multiply(0, i_and_g)
        quantise_weights(0, 1)
        multiply(0, f_and_o)
        turn_weights(1, 1)
        for m in range(1, FIRST_CHUNKS):
            for v in range(GATE_UNITS):
                group_weights(m, v, nc.vector.tensor_copy)
                if m + 1 < FIRST_CHUNKS:
                    turn_weights(m + 1, v)
            for v in range(GATE_UNITS):
                quantise_weights(m, v)
            if m == 1:
                multiply(1)


        jobs = [(b, UNIT, 1) for b in range(BLOCKS, 2 * BLOCKS, UNIT)]
        jobs += [(b, 1, b - LEAD) for b in range(2 * BLOCKS, Z_BLOCKS)]

        for n in range(STEPS):
            added, grouped, quantised = [
                [(b, count) for b, count, added_in in jobs if added_in == n - age] for age in range(3)
            ]

            for b, count in quantised:
                quantise_z(b, count)
            if 0 <= n - 1 < FIRST_SUMMED:
                add_cell(n - 1)
            for b, count in added:
                add_z(b, count)
            if 0 <= n - 2:
                copy_cell(n - 2)
            if FIRST_CHUNKS <= n + 2 < CHUNKS:
                for v in range(GATE_UNITS):
                    group_weights(n + 2, v, nc.vector.tensor_copy)
                for v in range(GATE_UNITS):
                    quantise_weights(n + 2, v)
            if 0 <= n - LAST_LAG:
                hidden(n - LAST_LAG)
            for b, count in grouped:
                group_z(b, count, nc.vector.tensor_copy)

            activate(n, I_GATE)
            activate(n, G_GATE)
            if n < STEPS - 1:
                multiply_gates(n, nc.gpsimd)
            activate(n, F_GATE)
            if 0 <= n - 3:
                tanh_cell(n - 3)
            activate(n, O_GATE)

            if 2 <= n + 1 < STEPS:
                multiply(n + 1, i_and_g)
                if n + 1 < STEPS - 1:
                    multiply(n + 1, f_and_o)
            if 0 <= n - 1:
                turn_cell(n - 1)
            if 0 <= n - 3:
                turn_sig_o(n - 3)
            if n + 1 == STEPS - 1:
                multiply(n + 1, f_and_o)
            if FIRST_CHUNKS <= n + 3 < CHUNKS:
                for v in range(GATE_UNITS):
                    turn_weights(n + 3, v)
            for b, count in added:
                turn_z(b, count)


        last = STEPS - 1
        multiply_gates(last, nc.vector)
        copy_cell(last - 1)
        turn_cell(last)
        hidden(last - 3)
        copy_cell(last)
        for n in range(last - 2, STEPS):
            turn_sig_o(n)
            tanh_cell(n)
            hidden(n)
